import numpy as np
import ml_dtypes


def mxq(x, axis, fmt="e4m3"):
    dtype, down = {"e4m3": (ml_dtypes.float8_e4m3fn, 7), "e5m2": (ml_dtypes.float8_e5m2, 14)}[fmt]
    v = np.moveaxis(np.asarray(x, np.float32).astype(ml_dtypes.bfloat16).astype(np.float64), axis, -1)
    blocks = v.reshape(v.shape[:-1] + (-1, 32))
    amax = np.abs(blocks).max(-1, keepdims=True)
    byte = np.maximum(np.where(amax > 0, np.frexp(amax)[1] - 1 + 127, 0) - down, 1)
    scale = np.exp2(byte - 127.0)
    codes = (blocks / scale).astype(np.float32).astype(dtype).astype(np.float64)
    return np.moveaxis((codes * scale).reshape(v.shape), -1, axis)


WIDE = False


def mx_kscale(k):
    if not WIDE:
        return np.ones(k)
    levels = np.array([10, -10, 5, -5, 0])
    if k % 512:
        return np.exp2(np.random.permutation(np.resize(levels, k // 32))).repeat(32)
    a = np.empty((k // 512, 16))
    for p in range(k // 512):
        a[p, :8] = np.random.permutation(np.resize(levels, 8))
        for g in range(8):
            far = levels[np.abs(levels - a[p, g]) >= 10]
            a[p, g + 8] = far[np.random.randint(len(far))]
    return np.exp2(a.ravel()).repeat(32)


BF16 = ml_dtypes.bfloat16


def bf(x):
    return np.asarray(x, np.float32).astype(BF16)


def f64(x):
    return np.asarray(x).astype(np.float64)


B, H = 1024, 1024


def sigmoid(v):
    return 1.0 / (1.0 + np.exp(-v))


def setup_inputs():
    s = mx_kscale(H)
    w = lambda: bf(np.random.standard_normal((H, H)) * 0.7 / np.sqrt(H) / s[None, :])
    b = lambda: bf(np.random.standard_normal(H) * 0.5)
    return {"inputs": bf(np.random.standard_normal((B, H)) * s),
            "short_term_memory": bf(np.random.standard_normal((B, H)) * s),
            "Wf": w(), "b_f": b(), "Wi": w(), "b_i": b(), "Wg": w(), "b_g": b(), "Wo": w(), "b_o": b()}


def reference(inputs, short_term_memory, Wf, b_f, Wi, b_i, Wg, b_g, Wo, b_o):
    z = f64(inputs) + f64(short_term_memory)
    zq = mxq(z, 1, "e4m3")
    c = sigmoid((zq @ mxq(f64(Wf), 1, "e4m3").T) + f64(b_f))
    c = c + sigmoid((zq @ mxq(f64(Wi), 1, "e4m3").T) + f64(b_i)) * np.tanh((zq @ mxq(f64(Wg), 1, "e4m3").T) + f64(b_g))
    h = np.tanh(c) * sigmoid((zq @ mxq(f64(Wo), 1, "e4m3").T) + f64(b_o))
    return np.stack((c, h))

@@ -1,0 +1,267 @@
+from contextlib import ExitStack
+
+import concourse.mybir as mybir
+from concourse.masks import make_identity
+
+F32 = mybir.dt.float32
+BF16 = mybir.dt.bfloat16
+U32 = mybir.dt.uint32
+U8 = mybir.dt.uint8
+FP8X4 = mybir.dt.float8_e4m3fn_x4
+FUNC = mybir.ActivationFunctionType
+ALU = mybir.AluOpType
+
+P = 128
+BATCH = 1024
+FEAT = 1024
+GATES = 4
+PACK = 4
+K_PASS = P * PACK
+PASSES = FEAT // K_PASS
+N_TILE = 512
+HALVES = BATCH // N_TILE
+HALF_BLOCKS = N_TILE // P
+ROWS = BATCH // P
+FEAT_BLOCKS = FEAT // P
+PSUM_BANKS = 8
+SECOND_HALF_FROM = 2
+
+FLOPS = 2 * BATCH * FEAT * GATES * FEAT
+
+
+def tile_lstmcell_pa_kernel(
+    tc, inputs, short_term_memory, Wf, b_f, Wi, b_i, Wg, b_g, Wo, b_o, out
+):
+    nc = tc.nc
+    weights = (Wi, Wg, Wf, Wo)
+    biases = (b_i, b_g, b_f, b_o)
+    gate_funcs = (FUNC.Sigmoid, FUNC.Tanh, FUNC.Sigmoid, FUNC.Sigmoid)
+
+    x_rows = inputs.rearrange("(p r) k -> p r k", r=ROWS)
+    s_rows = short_term_memory.rearrange("(p r) k -> p r k", r=ROWS)
+    out_rows = out.rearrange("s (p r) h -> s p r h", r=ROWS)
+
+    with ExitStack() as ctx:
+        ctx.enter_context(tc.manual_schedule())
+        const = ctx.enter_context(tc.tile_pool(name="const", bufs=1))
+        resident = ctx.enter_context(tc.tile_pool(name="resident", bufs=1))
+        grouped = ctx.enter_context(tc.tile_pool(name="grouped", bufs=2 * GATES))
+        work = ctx.enter_context(tc.tile_pool(name="work", bufs=2))
+        stores = ctx.enter_context(tc.tile_pool(name="stores", bufs=4))
+        psum = ctx.enter_context(tc.psum_pool(name="psum", bufs=PSUM_BANKS))
+
+        x_sb = [
+            resident.tile([P, HALF_BLOCKS, FEAT], BF16, name="x_sb%d" % half)
+            for half in range(HALVES)
+        ]
+        s_sb = [
+            resident.tile([P, HALF_BLOCKS, FEAT], BF16, name="s_sb%d" % half)
+            for half in range(HALVES)
+        ]
+        w_sb = [
+            resident.tile([P, GATES, FEAT], BF16, name="w_sb%d" % fb)
+            for fb in range(FEAT_BLOCKS)
+        ]
+        z_grouped = [
+            resident.tile([P, PASSES, N_TILE, PACK], BF16, name="z_grouped%d" % half, align_bytes=64)
+            for half in range(HALVES)
+        ]
+        z_codes = [
+            resident.tile([P, PASSES, N_TILE], U32, name="z_codes%d" % half, align_bytes=64)
+            for half in range(HALVES)
+        ]
+        z_scales = [
+            resident.tile([P, PASSES, N_TILE], U8, name="z_scales%d" % half, align_bytes=64)
+            for half in range(HALVES)
+        ]
+        w_codes = [
+            resident.tile([P, GATES, PASSES, P], U32, name="w_codes%d" % fb, align_bytes=64)
+            for fb in range(FEAT_BLOCKS)
+        ]
+        w_scales = [
+            resident.tile([P, GATES, PASSES, P], U8, name="w_scales%d" % fb, align_bytes=64)
+            for fb in range(FEAT_BLOCKS)
+        ]
+
+        def load_batch_half(half):
+            for j in range(HALF_BLOCKS):
+                nc.sync.dma_start(out=x_sb[half][:, j, :], in_=x_rows[:, HALF_BLOCKS * half + j, :])
+                nc.sync.dma_start(out=s_sb[half][:, j, :], in_=s_rows[:, HALF_BLOCKS * half + j, :])
+
+        def load_weight_block(fb):
+            for gate in range(GATES):
+                nc.sync.dma_start(
+                    out=w_sb[fb][:, gate, :], in_=weights[gate][fb * P : (fb + 1) * P, :]
+                )
+
+        load_batch_half(0)
+        for fb in range(FEAT_BLOCKS // 2):
+            load_weight_block(fb)
+        load_batch_half(1)
+        for fb in range(FEAT_BLOCKS // 2, FEAT_BLOCKS):
+            load_weight_block(fb)
+
+        bias_rows = const.tile([P, P], BF16)
+        nc.vector.memset(bias_rows[:], 0.0)
+        for gate in range(GATES):
+            nc.scalar.dma_start(
+                out=bias_rows[gate * FEAT_BLOCKS : (gate + 1) * FEAT_BLOCKS, :],
+                in_=biases[gate].rearrange("(r c) -> r c", c=P),
+            )
+        warm = const.tile([P, 1], F32)
+        nc.vector.memset(warm[:], 0.0)
+        nc.scalar.activation(out=warm[:], in_=warm[:], func=FUNC.Sigmoid)
+
+        ident_bf = const.tile([P, P], BF16)
+        make_identity(nc, ident_bf[:])
+        ident_f32 = const.tile([P, P], F32)
+        make_identity(nc, ident_f32[:])
+
+        def copy_out(piece, out_ap, in_ap):
+            if piece % 2 == 0:
+                nc.scalar.copy(out=out_ap, in_=in_ap)
+            else:
+                nc.vector.tensor_copy(out=out_ap, in_=in_ap)
+
+        def flip_bias():
+            bias_t = psum.tile([P, P], BF16, tag="bank")
+            nc.tensor.transpose(bias_t[:], bias_rows[:], ident_bf[:])
+            bias_sb = const.tile([P, GATES * FEAT_BLOCKS], F32)
+            nc.vector.tensor_copy(out=bias_sb[:], in_=bias_t[:, 0 : GATES * FEAT_BLOCKS])
+            return bias_sb
+
+        def flip_z_block(half, j):
+            x_quads = x_sb[half][:, j, :].rearrange("p (w t) -> p t w", t=PACK)
+            s_quads = s_sb[half][:, j, :].rearrange("p (w t) -> p t w", t=PACK)
+            for g in range(PASSES):
+                z_t = psum.tile([P, PACK, P], F32, tag="bank")
+                for t in range(PACK):
+                    quads = slice(g * P, (g + 1) * P)
+                    nc.tensor.matmul(
+                        z_t[:, t, :], lhsT=x_quads[:, t, quads], rhs=ident_bf[:],
+                        start=True, stop=False,
+                    )
+                    nc.tensor.matmul(
+                        z_t[:, t, :], lhsT=s_quads[:, t, quads], rhs=ident_bf[:],
+                        start=False, stop=True,
+                    )
+                copy_out(
+                    g,
+                    z_grouped[half][:, g, j * P : (j + 1) * P, :],
+                    z_t[:].rearrange("p t b -> p b t"),
+                )
+
+        def quantise_z(half):
+            for g in range(PASSES):
+                nc.vector.quantize_mx(
+                    out=z_codes[half][:, g, :].bitcast(FP8X4),
+                    scales=z_scales[half][:, g, :],
+                    in_=z_grouped[half][:, g, :, :].rearrange("p b t -> p (b t)"),
+                )
+
+        def flip_weight(fb, gate):
+            w_words = w_sb[fb][:, gate, :].bitcast(F32).rearrange("p (g w u) -> p g u w", g=PASSES, u=2)
+            w_t = psum.tile([P, PASSES * 2, P], F32, tag="bank")
+            for plane in range(PASSES * 2):
+                nc.tensor.transpose(
+                    w_t[:, plane, :], w_words[:, plane // 2, plane % 2, :], ident_f32[:]
+                )
+            w_grouped = grouped.tile([P, PASSES, P * PACK], BF16, align_bytes=64)
+            copy_out(
+                gate,
+                w_grouped[:].bitcast(F32).rearrange("p g (n u) -> p g n u", u=2),
+                w_t[:].rearrange("p (g u) n -> p g n u", u=2),
+            )
+            return w_grouped
+
+        def quantise_weight(fb, gate, w_grouped):
+            nc.vector.quantize_mx(
+                out=w_codes[fb][:, gate, :, :].rearrange("p g n -> p (g n)").bitcast(FP8X4),
+                scales=w_scales[fb][:, gate, :, :].rearrange("p g n -> p (g n)"),
+                in_=w_grouped[:].rearrange("p g c -> p (g c)"),
+            )
+
+        def gates(half, fb):
+            acted = []
+            for gate in range(GATES):
+                acc = psum.tile([P, N_TILE], F32, tag="bank")
+                for g in range(PASSES):
+                    nc.tensor.matmul_mx(
+                        out=acc[:],
+                        lhsT=w_codes[fb][:, gate, g, :].bitcast(FP8X4),
+                        lhsT_scale=w_scales[fb][:, gate, g, :],
+                        rhs=z_codes[half][:, g, :].bitcast(FP8X4),
+                        rhs_scale=z_scales[half][:, g, :],
+                        start=(g == 0),
+                        stop=(g == PASSES - 1),
+                    )
+                gate_sb = work.tile(
+                    [P, N_TILE], F32, name="gate%d" % gate, bufs=(3 if gate == GATES - 1 else 2)
+                )
+                column = gate * FEAT_BLOCKS + fb
+                nc.scalar.activation(
+                    out=gate_sb[:], in_=acc[:], func=gate_funcs[gate],
+                    bias=bias_sb[:, column : column + 1], scale=1.0,
+                )
+                acted.append(gate_sb)
+            i_sb, g_sb, f_sb, o_sb = acted
+            ig_sb = work.tile([P, N_TILE], F32)
+            nc.vector.tensor_tensor(out=ig_sb[:], in0=i_sb[:], in1=g_sb[:], op=ALU.mult)
+            c_sb = work.tile([P, N_TILE], F32)
+            nc.vector.tensor_tensor(out=c_sb[:], in0=f_sb[:], in1=ig_sb[:], op=ALU.add)
+            return half, fb, c_sb, o_sb
+
+        def turn_c(half, fb, c_sb, o_sb):
+            c_t = psum.tile([P, HALF_BLOCKS, P], F32, tag="bank")
+            for j in range(HALF_BLOCKS):
+                nc.tensor.transpose(c_t[:, j, :], c_sb[:, j * P : (j + 1) * P], ident_f32[:])
+            c_out = stores.tile([P, HALF_BLOCKS, P], F32)
+            nc.vector.tensor_copy(out=c_out[:], in_=c_t[:])
+            rows = slice(HALF_BLOCKS * half, HALF_BLOCKS * (half + 1))
+            nc.sync.dma_start(out=out_rows[0, :, rows, fb * P : (fb + 1) * P], in_=c_out[:])
+            return half, fb, c_out, o_sb
+
+        def finish(half, fb, c_out, o_sb):
+            o_t = psum.tile([P, HALF_BLOCKS, P], F32, tag="bank")
+            for j in range(HALF_BLOCKS):
+                nc.tensor.transpose(o_t[:, j, :], o_sb[:, j * P : (j + 1) * P], ident_f32[:])
+            tanh_c = work.tile([P, HALF_BLOCKS, P], F32)
+            nc.scalar.activation(out=tanh_c[:], in_=c_out[:], func=FUNC.Tanh)
+            h_out = stores.tile([P, HALF_BLOCKS, P], F32)
+            nc.vector.tensor_tensor(out=h_out[:], in0=o_t[:], in1=tanh_c[:], op=ALU.mult)
+            rows = slice(HALF_BLOCKS * half, HALF_BLOCKS * (half + 1))
+            nc.sync.dma_start(out=out_rows[1, :, rows, fb * P : (fb + 1) * P], in_=h_out[:])
+
+        for j in range(HALF_BLOCKS):
+            flip_z_block(0, j)
+        quantise_z(0)
+        bias_sb = flip_bias()
+        for gate in range(GATES):
+            quantise_weight(0, gate, flip_weight(0, gate))
+        flipped = [flip_weight(1, gate) for gate in range(GATES)]
+        for gate in range(GATES):
+            quantise_weight(1, gate, flipped[gate])
+
+        acted = None
+        turned = None
+        for half in range(HALVES):
+            for fb in range(FEAT_BLOCKS):
+                fresh = gates(half, fb)
+                newly_turned = turn_c(*acted) if acted is not None else None
+                if turned is not None:
+                    finish(*turned)
+                acted, turned = fresh, newly_turned
+                if half == 0:
+                    ahead = fb + 2 if fb + 2 < FEAT_BLOCKS else None
+                    if ahead is not None:
+                        flipped = [flip_weight(ahead, gate) for gate in range(GATES)]
+                    if 0 <= fb - SECOND_HALF_FROM < HALF_BLOCKS:
+                        flip_z_block(1, fb - SECOND_HALF_FROM)
+                    if ahead is not None:
+                        for gate in range(GATES):
+                            quantise_weight(ahead, gate, flipped[gate])
+                    if fb - SECOND_HALF_FROM == HALF_BLOCKS:
+                        quantise_z(1)
+        newly_turned = turn_c(*acted)
+        finish(*turned)
+        finish(*newly_turned)

@@ -130,26 +130,32 @@ def tile_lstmcell_pa_kernel(
             nc.vector.tensor_copy(out=bias_sb[:], in_=bias_t[:, 0 : GATES * FEAT_BLOCKS])
             return bias_sb
 
-        def flip_z_block(half, j):
-            x_quads = x_sb[half][:, j, :].rearrange("p (w t) -> p t w", t=PACK)
-            s_quads = s_sb[half][:, j, :].rearrange("p (w t) -> p t w", t=PACK)
-            for g in range(PASSES):
-                z_t = psum.tile([P, PACK, P], F32, tag="bank")
-                for t in range(PACK):
-                    quads = slice(g * P, (g + 1) * P)
-                    nc.tensor.matmul(
-                        z_t[:, t, :], lhsT=x_quads[:, t, quads], rhs=ident_bf[:],
-                        start=True, stop=False,
-                    )
-                    nc.tensor.matmul(
-                        z_t[:, t, :], lhsT=s_quads[:, t, quads], rhs=ident_bf[:],
-                        start=False, stop=True,
-                    )
-                copy_out(
-                    g,
-                    z_grouped[half][:, g, j * P : (j + 1) * P, :],
-                    z_t[:].rearrange("p t b -> p b t"),
+        def flip_words(src):
+            words = src.bitcast(F32).rearrange("p (g w u) -> p g u w", g=PASSES, u=2)
+            flipped = psum.tile([P, PASSES * 2, P], F32, tag="bank")
+            for plane in range(PASSES * 2):
+                nc.tensor.transpose(
+                    flipped[:, plane, :], words[:, plane // 2, plane % 2, :], ident_f32[:]
                 )
+            return flipped
+
+        def interleave(piece, grouped_words, flipped):
+            copy_out(piece, grouped_words, flipped[:].rearrange("p (g u) n -> p g n u", u=2))
+
+        def add_z_block(half, j):
+            nc.vector.tensor_tensor(
+                out=x_sb[half][:, j, :], in0=x_sb[half][:, j, :], in1=s_sb[half][:, j, :], op=ALU.add
+            )
+
+        def flip_z_block(half, j):
+            z_t = flip_words(x_sb[half][:, j, :])
+            interleave(
+                0,
+                z_grouped[half][:, :, j * P : (j + 1) * P, :]
+                .rearrange("p g b t -> p g (b t)").bitcast(F32)
+                .rearrange("p g (n u) -> p g n u", u=2),
+                z_t,
+            )
 
         def quantise_z(half):
             for g in range(PASSES):
@@ -160,17 +166,10 @@ def tile_lstmcell_pa_kernel(
                 )
 
         def flip_weight(fb, gate):
-            w_words = w_sb[fb][:, gate, :].bitcast(F32).rearrange("p (g w u) -> p g u w", g=PASSES, u=2)
-            w_t = psum.tile([P, PASSES * 2, P], F32, tag="bank")
-            for plane in range(PASSES * 2):
-                nc.tensor.transpose(
-                    w_t[:, plane, :], w_words[:, plane // 2, plane % 2, :], ident_f32[:]
-                )
+            w_t = flip_words(w_sb[fb][:, gate, :])
             w_grouped = grouped.tile([P, PASSES, P * PACK], BF16, align_bytes=64)
-            copy_out(
-                gate,
-                w_grouped[:].bitcast(F32).rearrange("p g (n u) -> p g n u", u=2),
-                w_t[:].rearrange("p (g u) n -> p g n u", u=2),
+            interleave(
+                gate, w_grouped[:].bitcast(F32).rearrange("p g (n u) -> p g n u", u=2), w_t
             )
             return w_grouped
 
@@ -233,6 +232,7 @@ def tile_lstmcell_pa_kernel(
             nc.sync.dma_start(out=out_rows[1, :, rows, fb * P : (fb + 1) * P], in_=h_out[:])
 
         for j in range(HALF_BLOCKS):
+            add_z_block(0, j)
             flip_z_block(0, j)
         quantise_z(0)
         bias_sb = flip_bias()
@@ -255,6 +255,8 @@ def tile_lstmcell_pa_kernel(
                     ahead = fb + 2 if fb + 2 < FEAT_BLOCKS else None
                     if ahead is not None:
                         flipped = [flip_weight(ahead, gate) for gate in range(GATES)]
+                    if 0 <= fb + 1 - SECOND_HALF_FROM < HALF_BLOCKS:
+                        add_z_block(1, fb + 1 - SECOND_HALF_FROM)
                     if 0 <= fb - SECOND_HALF_FROM < HALF_BLOCKS:
                         flip_z_block(1, fb - SECOND_HALF_FROM)
                     if ahead is not None:

@@ -26,6 +26,9 @@ FEAT_BLOCKS = FEAT // P
 PSUM_BANKS = 8
 SECOND_HALF_FROM = 2
 
+EVEN_SHARES = ("scalar", "vector", "scalar", "vector")
+PIPELINE_SHARES = ("vector", "scalar", "scalar", "scalar")
+
 FLOPS = 2 * BATCH * FEAT * GATES * FEAT
 
 
@@ -45,7 +48,7 @@ def tile_lstmcell_pa_kernel(
         ctx.enter_context(tc.manual_schedule())
         const = ctx.enter_context(tc.tile_pool(name="const", bufs=1))
         resident = ctx.enter_context(tc.tile_pool(name="resident", bufs=1))
-        grouped = ctx.enter_context(tc.tile_pool(name="grouped", bufs=2 * GATES))
+        grouped = ctx.enter_context(tc.tile_pool(name="grouped", bufs=2))
         work = ctx.enter_context(tc.tile_pool(name="work", bufs=2))
         stores = ctx.enter_context(tc.tile_pool(name="stores", bufs=4))
         psum = ctx.enter_context(tc.psum_pool(name="psum", bufs=PSUM_BANKS))
@@ -117,8 +120,8 @@ def tile_lstmcell_pa_kernel(
         ident_f32 = const.tile([P, P], F32)
         make_identity(nc, ident_f32[:])
 
-        def copy_out(piece, out_ap, in_ap):
-            if piece % 2 == 0:
+        def copy_out(engine, out_ap, in_ap):
+            if engine == "scalar":
                 nc.scalar.copy(out=out_ap, in_=in_ap)
             else:
                 nc.vector.tensor_copy(out=out_ap, in_=in_ap)
@@ -139,8 +142,8 @@ def tile_lstmcell_pa_kernel(
                 )
             return flipped
 
-        def interleave(piece, grouped_words, flipped):
-            copy_out(piece, grouped_words, flipped[:].rearrange("p (g u) n -> p g n u", u=2))
+        def interleave(engine, grouped_words, flipped):
+            copy_out(engine, grouped_words, flipped[:].rearrange("p (g u) n -> p g n u", u=2))
 
         def add_z_block(half, j):
             nc.vector.tensor_tensor(
@@ -150,35 +153,43 @@ def tile_lstmcell_pa_kernel(
         def flip_z_block(half, j):
             z_t = flip_words(x_sb[half][:, j, :])
             interleave(
-                0,
+                "scalar",
                 z_grouped[half][:, :, j * P : (j + 1) * P, :]
                 .rearrange("p g b t -> p g (b t)").bitcast(F32)
                 .rearrange("p g (n u) -> p g n u", u=2),
                 z_t,
             )
 
-        def quantise_z(half):
+        def quantise_z(half, j, blocks):
+            cols = slice(j * P, (j + blocks) * P)
             for g in range(PASSES):
                 nc.vector.quantize_mx(
-                    out=z_codes[half][:, g, :].bitcast(FP8X4),
-                    scales=z_scales[half][:, g, :],
-                    in_=z_grouped[half][:, g, :, :].rearrange("p b t -> p (b t)"),
+                    out=z_codes[half][:, g, cols].bitcast(FP8X4),
+                    scales=z_scales[half][:, g, cols],
+                    in_=z_grouped[half][:, g, cols, :].rearrange("p b t -> p (b t)"),
                 )
 
-        def flip_weight(fb, gate):
+        def flip_weight(engine, w_grouped, fb, gate):
             w_t = flip_words(w_sb[fb][:, gate, :])
-            w_grouped = grouped.tile([P, PASSES, P * PACK], BF16, align_bytes=64)
             interleave(
-                gate, w_grouped[:].bitcast(F32).rearrange("p g (n u) -> p g n u", u=2), w_t
+                engine,
+                w_grouped[:, gate, :, :].bitcast(F32).rearrange("p g (n u) -> p g n u", u=2),
+                w_t,
             )
-            return w_grouped
 
-        def quantise_weight(fb, gate, w_grouped):
+        def quantise_weight(fb, w_grouped, gate, count):
+            some = slice(gate, gate + count)
             nc.vector.quantize_mx(
-                out=w_codes[fb][:, gate, :, :].rearrange("p g n -> p (g n)").bitcast(FP8X4),
-                scales=w_scales[fb][:, gate, :, :].rearrange("p g n -> p (g n)"),
-                in_=w_grouped[:].rearrange("p g c -> p (g c)"),
+                out=w_codes[fb][:, some, :, :].rearrange("p a g n -> p (a g n)").bitcast(FP8X4),
+                scales=w_scales[fb][:, some, :, :].rearrange("p a g n -> p (a g n)"),
+                in_=w_grouped[:, some, :, :].rearrange("p a g c -> p (a g c)"),
             )
+
+        def flip_weight_block(fb, engines):
+            w_grouped = grouped.tile([P, GATES, PASSES, P * PACK], BF16, align_bytes=64)
+            for gate in range(GATES):
+                flip_weight(engines[gate], w_grouped, fb, gate)
+            return w_grouped
 
         def gates(half, fb):
             acted = []
@@ -233,14 +244,20 @@ def tile_lstmcell_pa_kernel(
 
         for j in range(HALF_BLOCKS):
             add_z_block(0, j)
+            if j > 1:
+                quantise_z(0, j - 2, 1)
             flip_z_block(0, j)
-        quantise_z(0)
+        quantise_z(0, HALF_BLOCKS - 2, 1)
+        w_grouped = grouped.tile([P, GATES, PASSES, P * PACK], BF16, align_bytes=64)
+        flip_weight("scalar", w_grouped, 0, 0)
+        quantise_z(0, HALF_BLOCKS - 1, 1)
         bias_sb = flip_bias()
-        for gate in range(GATES):
-            quantise_weight(0, gate, flip_weight(0, gate))
-        flipped = [flip_weight(1, gate) for gate in range(GATES)]
-        for gate in range(GATES):
-            quantise_weight(1, gate, flipped[gate])
+        for gate in range(1, GATES):
+            flip_weight(EVEN_SHARES[gate], w_grouped, 0, gate)
+            quantise_weight(0, w_grouped, gate - 1, 1)
+        quantise_weight(0, w_grouped, GATES - 1, 1)
+        w_grouped = flip_weight_block(1, EVEN_SHARES)
+        quantise_weight(1, w_grouped, 0, GATES)
 
         acted = None
         turned = None
@@ -253,17 +270,16 @@ def tile_lstmcell_pa_kernel(
                 acted, turned = fresh, newly_turned
                 if half == 0:
                     ahead = fb + 2 if fb + 2 < FEAT_BLOCKS else None
-                    if ahead is not None:
-                        flipped = [flip_weight(ahead, gate) for gate in range(GATES)]
                     if 0 <= fb + 1 - SECOND_HALF_FROM < HALF_BLOCKS:
                         add_z_block(1, fb + 1 - SECOND_HALF_FROM)
+                    if ahead is not None:
+                        w_grouped = flip_weight_block(ahead, PIPELINE_SHARES)
                     if 0 <= fb - SECOND_HALF_FROM < HALF_BLOCKS:
                         flip_z_block(1, fb - SECOND_HALF_FROM)
                     if ahead is not None:
-                        for gate in range(GATES):
-                            quantise_weight(ahead, gate, flipped[gate])
+                        quantise_weight(ahead, w_grouped, 0, GATES)
                     if fb - SECOND_HALF_FROM == HALF_BLOCKS:
-                        quantise_z(1)
+                        quantise_z(1, 0, HALF_BLOCKS)
         newly_turned = turn_c(*acted)
         finish(*turned)
         finish(*newly_turned)

@@ -27,7 +27,10 @@ PSUM_BANKS = 8
 SECOND_HALF_FROM = 2
 
 EVEN_SHARES = ("scalar", "vector", "scalar", "vector")
-PIPELINE_SHARES = ("vector", "scalar", "scalar", "scalar")
+PIPELINE_SHARES = ("vector", "scalar", "vector", "scalar")
+
+TAIL_PARTS = 2
+TAIL_BLOCKS = HALF_BLOCKS // TAIL_PARTS
 
 FLOPS = 2 * BATCH * FEAT * GATES * FEAT
 
@@ -191,7 +194,7 @@ def tile_lstmcell_pa_kernel(
                 flip_weight(engines[gate], w_grouped, fb, gate)
             return w_grouped
 
-        def gates(half, fb):
+        def gates(half, fb, parts):
             acted = []
             for gate in range(GATES):
                 acc = psum.tile([P, N_TILE], F32, tag="bank")
@@ -218,7 +221,11 @@ def tile_lstmcell_pa_kernel(
             ig_sb = work.tile([P, N_TILE], F32)
             nc.vector.tensor_tensor(out=ig_sb[:], in0=i_sb[:], in1=g_sb[:], op=ALU.mult)
             c_sb = work.tile([P, N_TILE], F32)
-            nc.vector.tensor_tensor(out=c_sb[:], in0=f_sb[:], in1=ig_sb[:], op=ALU.add)
+            for part in range(parts):
+                cols = slice(part * N_TILE // parts, (part + 1) * N_TILE // parts)
+                nc.vector.tensor_tensor(
+                    out=c_sb[:, cols], in0=f_sb[:, cols], in1=ig_sb[:, cols], op=ALU.add
+                )
             return half, fb, c_sb, o_sb
 
         def turn_c(half, fb, c_sb, o_sb):
@@ -242,6 +249,46 @@ def tile_lstmcell_pa_kernel(
             rows = slice(HALF_BLOCKS * half, HALF_BLOCKS * (half + 1))
             nc.sync.dma_start(out=out_rows[1, :, rows, fb * P : (fb + 1) * P], in_=h_out[:])
 
+        def start_last(half, fb, c_sb, o_sb):
+            c_parts = []
+            for part in range(TAIL_PARTS):
+                c_t = psum.tile([P, TAIL_BLOCKS, P], F32, tag="bank")
+                for j in range(TAIL_BLOCKS):
+                    block = part * TAIL_BLOCKS + j
+                    nc.tensor.transpose(
+                        c_t[:, j, :], c_sb[:, block * P : (block + 1) * P], ident_f32[:]
+                    )
+                c_parts.append(c_t)
+            o_t = psum.tile([P, HALF_BLOCKS, P], F32, tag="bank")
+            for j in range(HALF_BLOCKS):
+                nc.tensor.transpose(o_t[:, j, :], o_sb[:, j * P : (j + 1) * P], ident_f32[:])
+            tanh_parts = []
+            for part in range(TAIL_PARTS):
+                tanh_c = work.tile([P, TAIL_BLOCKS, P], F32, name="tanh_last")
+                nc.scalar.activation(out=tanh_c[:], in_=c_parts[part][:], func=FUNC.Tanh)
+                tanh_parts.append(tanh_c)
+            for part in range(TAIL_PARTS):
+                blocks = slice(part * TAIL_BLOCKS, (part + 1) * TAIL_BLOCKS)
+                h_out = stores.tile([P, TAIL_BLOCKS, P], F32, name="h_last", bufs=2)
+                nc.vector.tensor_tensor(
+                    out=h_out[:], in0=o_t[:, blocks, :], in1=tanh_parts[part][:], op=ALU.mult
+                )
+                store_part(1, half, fb, part, h_out)
+            return half, fb, c_parts
+
+        def store_last_c(half, fb, c_parts):
+            for part in range(TAIL_PARTS):
+                c_out = stores.tile([P, TAIL_BLOCKS, P], F32, name="c_last", bufs=2)
+                nc.scalar.copy(out=c_out[:], in_=c_parts[part][:])
+                store_part(0, half, fb, part, c_out)
+
+        def store_part(which, half, fb, part, tile):
+            first = HALF_BLOCKS * half + TAIL_BLOCKS * part
+            nc.sync.dma_start(
+                out=out_rows[which, :, first : first + TAIL_BLOCKS, fb * P : (fb + 1) * P],
+                in_=tile[:],
+            )
+
         for j in range(HALF_BLOCKS):
             add_z_block(0, j)
             if j > 1:
@@ -263,7 +310,8 @@ def tile_lstmcell_pa_kernel(
         turned = None
         for half in range(HALVES):
             for fb in range(FEAT_BLOCKS):
-                fresh = gates(half, fb)
+                last = half == HALVES - 1 and fb == FEAT_BLOCKS - 1
+                fresh = gates(half, fb, TAIL_PARTS if last else 1)
                 newly_turned = turn_c(*acted) if acted is not None else None
                 if turned is not None:
                     finish(*turned)
@@ -280,6 +328,6 @@ def tile_lstmcell_pa_kernel(
                         quantise_weight(ahead, w_grouped, 0, GATES)
                     if fb - SECOND_HALF_FROM == HALF_BLOCKS:
                         quantise_z(1, 0, HALF_BLOCKS)
-        newly_turned = turn_c(*acted)
+        c_parts = start_last(*acted)
         finish(*turned)
-        finish(*newly_turned)
+        store_last_c(*c_parts)

@@ -24,10 +24,10 @@ HALF_BLOCKS = N_TILE // P
 ROWS = BATCH // P
 FEAT_BLOCKS = FEAT // P
 PSUM_BANKS = 8
-SECOND_HALF_FROM = 2
+Z_STEP = FEAT_BLOCKS - 2
 
 EVEN_SHARES = ("scalar", "vector", "scalar", "vector")
-PIPELINE_SHARES = ("vector", "scalar", "vector", "scalar")
+PIPELINE_SHARES = ("vector", "scalar", "scalar", "scalar")
 
 TAIL_PARTS = 2
 TAIL_BLOCKS = HALF_BLOCKS // TAIL_PARTS
@@ -101,10 +101,10 @@ def tile_lstmcell_pa_kernel(
                 )
 
         load_batch_half(0)
-        for fb in range(FEAT_BLOCKS // 2):
+        for fb in range(Z_STEP - 1):
             load_weight_block(fb)
         load_batch_half(1)
-        for fb in range(FEAT_BLOCKS // 2, FEAT_BLOCKS):
+        for fb in range(Z_STEP - 1, FEAT_BLOCKS):
             load_weight_block(fb)
 
         bias_rows = const.tile([P, P], BF16)
@@ -153,10 +153,10 @@ def tile_lstmcell_pa_kernel(
                 out=x_sb[half][:, j, :], in0=x_sb[half][:, j, :], in1=s_sb[half][:, j, :], op=ALU.add
             )
 
-        def flip_z_block(half, j):
+        def flip_z_block(engine, half, j):
             z_t = flip_words(x_sb[half][:, j, :])
             interleave(
-                "scalar",
+                engine,
                 z_grouped[half][:, :, j * P : (j + 1) * P, :]
                 .rearrange("p g b t -> p g (b t)").bitcast(F32)
                 .rearrange("p g (n u) -> p g n u", u=2),
@@ -194,7 +194,7 @@ def tile_lstmcell_pa_kernel(
                 flip_weight(engines[gate], w_grouped, fb, gate)
             return w_grouped
 
-        def gates(half, fb, parts):
+        def gates(half, fb, parts, between):
             acted = []
             for gate in range(GATES):
                 acc = psum.tile([P, N_TILE], F32, tag="bank")
@@ -220,6 +220,7 @@ def tile_lstmcell_pa_kernel(
             i_sb, g_sb, f_sb, o_sb = acted
             ig_sb = work.tile([P, N_TILE], F32)
             nc.vector.tensor_tensor(out=ig_sb[:], in0=i_sb[:], in1=g_sb[:], op=ALU.mult)
+            between()
             c_sb = work.tile([P, N_TILE], F32)
             for part in range(parts):
                 cols = slice(part * N_TILE // parts, (part + 1) * N_TILE // parts)
@@ -293,7 +294,7 @@ def tile_lstmcell_pa_kernel(
             add_z_block(0, j)
             if j > 1:
                 quantise_z(0, j - 2, 1)
-            flip_z_block(0, j)
+            flip_z_block("scalar", 0, j)
         quantise_z(0, HALF_BLOCKS - 2, 1)
         w_grouped = grouped.tile([P, GATES, PASSES, P * PACK], BF16, align_bytes=64)
         flip_weight("scalar", w_grouped, 0, 0)
@@ -303,31 +304,36 @@ def tile_lstmcell_pa_kernel(
             flip_weight(EVEN_SHARES[gate], w_grouped, 0, gate)
             quantise_weight(0, w_grouped, gate - 1, 1)
         quantise_weight(0, w_grouped, GATES - 1, 1)
-        w_grouped = flip_weight_block(1, EVEN_SHARES)
-        quantise_weight(1, w_grouped, 0, GATES)
+        waiting = flip_weight_block(1, EVEN_SHARES)
 
         acted = None
         turned = None
         for half in range(HALVES):
             for fb in range(FEAT_BLOCKS):
                 last = half == HALVES - 1 and fb == FEAT_BLOCKS - 1
-                fresh = gates(half, fb, TAIL_PARTS if last else 1)
+                z_block = fb - (Z_STEP - HALF_BLOCKS + 1) if half == 0 else -1
+                grouped_before, waiting = waiting, None
+                if grouped_before is not None:
+                    quantise_weight(fb + 1, grouped_before, 0, GATES // 2)
+                if 0 <= z_block < HALF_BLOCKS:
+                    add_z_block(1, z_block)
+                if half == 0 and fb == Z_STEP + 1:
+                    quantise_z(1, 0, HALF_BLOCKS)
+
+                def quantise_the_rest():
+                    if grouped_before is not None:
+                        quantise_weight(fb + 1, grouped_before, GATES // 2, GATES // 2)
+
+                fresh = gates(half, fb, TAIL_PARTS if last else 1, quantise_the_rest)
                 newly_turned = turn_c(*acted) if acted is not None else None
                 if turned is not None:
                     finish(*turned)
                 acted, turned = fresh, newly_turned
-                if half == 0:
-                    ahead = fb + 2 if fb + 2 < FEAT_BLOCKS else None
-                    if 0 <= fb + 1 - SECOND_HALF_FROM < HALF_BLOCKS:
-                        add_z_block(1, fb + 1 - SECOND_HALF_FROM)
-                    if ahead is not None:
-                        w_grouped = flip_weight_block(ahead, PIPELINE_SHARES)
-                    if 0 <= fb - SECOND_HALF_FROM < HALF_BLOCKS:
-                        flip_z_block(1, fb - SECOND_HALF_FROM)
-                    if ahead is not None:
-                        quantise_weight(ahead, w_grouped, 0, GATES)
-                    if fb - SECOND_HALF_FROM == HALF_BLOCKS:
-                        quantise_z(1, 0, HALF_BLOCKS)
+                if half == 0 and fb + 2 < FEAT_BLOCKS:
+                    waiting = flip_weight_block(fb + 2, PIPELINE_SHARES)
+                if half == 0 and fb == Z_STEP:
+                    for j in range(HALF_BLOCKS):
+                        flip_z_block(PIPELINE_SHARES[j], 1, j)
         c_parts = start_last(*acted)
         finish(*turned)
         store_last_c(*c_parts)

@@ -188,39 +188,38 @@ def tile_lstmcell_pa_kernel(
                 in_=w_grouped[:, some, :, :].rearrange("p a g c -> p (a g c)"),
             )
 
-        def flip_weight_block(fb, engines):
-            w_grouped = grouped.tile([P, GATES, PASSES, P * PACK], BF16, align_bytes=64)
-            for gate in range(GATES):
-                flip_weight(engines[gate], w_grouped, fb, gate)
-            return w_grouped
+        def gate_of(half, fb, gate):
+            acc = psum.tile([P, N_TILE], F32, tag="bank")
+            for g in range(PASSES):
+                nc.tensor.matmul_mx(
+                    out=acc[:],
+                    lhsT=w_codes[fb][:, gate, g, :].bitcast(FP8X4),
+                    lhsT_scale=w_scales[fb][:, gate, g, :],
+                    rhs=z_codes[half][:, g, :].bitcast(FP8X4),
+                    rhs_scale=z_scales[half][:, g, :],
+                    start=(g == 0),
+                    stop=(g == PASSES - 1),
+                )
+            gate_sb = work.tile(
+                [P, N_TILE], F32, name="gate%d" % gate, bufs=(3 if gate == GATES - 1 else 2)
+            )
+            column = gate * FEAT_BLOCKS + fb
+            nc.scalar.activation(
+                out=gate_sb[:], in_=acc[:], func=gate_funcs[gate],
+                bias=bias_sb[:, column : column + 1], scale=1.0,
+            )
+            return gate_sb
 
-        def gates(half, fb, parts, between):
-            acted = []
-            for gate in range(GATES):
-                acc = psum.tile([P, N_TILE], F32, tag="bank")
-                for g in range(PASSES):
-                    nc.tensor.matmul_mx(
-                        out=acc[:],
-                        lhsT=w_codes[fb][:, gate, g, :].bitcast(FP8X4),
-                        lhsT_scale=w_scales[fb][:, gate, g, :],
-                        rhs=z_codes[half][:, g, :].bitcast(FP8X4),
-                        rhs_scale=z_scales[half][:, g, :],
-                        start=(g == 0),
-                        stop=(g == PASSES - 1),
-                    )
-                gate_sb = work.tile(
-                    [P, N_TILE], F32, name="gate%d" % gate, bufs=(3 if gate == GATES - 1 else 2)
-                )
-                column = gate * FEAT_BLOCKS + fb
-                nc.scalar.activation(
-                    out=gate_sb[:], in_=acc[:], func=gate_funcs[gate],
-                    bias=bias_sb[:, column : column + 1], scale=1.0,
-                )
-                acted.append(gate_sb)
-            i_sb, g_sb, f_sb, o_sb = acted
+        def first_gates(half, fb):
+            i_sb = gate_of(half, fb, 0)
+            g_sb = gate_of(half, fb, 1)
             ig_sb = work.tile([P, N_TILE], F32)
             nc.vector.tensor_tensor(out=ig_sb[:], in0=i_sb[:], in1=g_sb[:], op=ALU.mult)
-            between()
+            return ig_sb
+
+        def last_gates(half, fb, ig_sb, parts):
+            f_sb = gate_of(half, fb, 2)
+            o_sb = gate_of(half, fb, 3)
             c_sb = work.tile([P, N_TILE], F32)
             for part in range(parts):
                 cols = slice(part * N_TILE // parts, (part + 1) * N_TILE // parts)
@@ -229,26 +228,33 @@ def tile_lstmcell_pa_kernel(
                 )
             return half, fb, c_sb, o_sb
 
-        def turn_c(half, fb, c_sb, o_sb):
-            c_t = psum.tile([P, HALF_BLOCKS, P], F32, tag="bank")
+        def flip_back(src):
+            flipped = psum.tile([P, HALF_BLOCKS, P], F32, tag="bank")
             for j in range(HALF_BLOCKS):
-                nc.tensor.transpose(c_t[:, j, :], c_sb[:, j * P : (j + 1) * P], ident_f32[:])
+                nc.tensor.transpose(flipped[:, j, :], src[:, j * P : (j + 1) * P], ident_f32[:])
+            return flipped
+
+        def store(which, half, fb, tile):
+            rows = slice(HALF_BLOCKS * half, HALF_BLOCKS * (half + 1))
+            nc.sync.dma_start(out=out_rows[which, :, rows, fb * P : (fb + 1) * P], in_=tile[:])
+
+        def turn_c(half, fb, c_sb, o_sb):
+            c_t = flip_back(c_sb)
             c_out = stores.tile([P, HALF_BLOCKS, P], F32)
             nc.vector.tensor_copy(out=c_out[:], in_=c_t[:])
-            rows = slice(HALF_BLOCKS * half, HALF_BLOCKS * (half + 1))
-            nc.sync.dma_start(out=out_rows[0, :, rows, fb * P : (fb + 1) * P], in_=c_out[:])
+            store(0, half, fb, c_out)
             return half, fb, c_out, o_sb
 
-        def finish(half, fb, c_out, o_sb):
-            o_t = psum.tile([P, HALF_BLOCKS, P], F32, tag="bank")
-            for j in range(HALF_BLOCKS):
-                nc.tensor.transpose(o_t[:, j, :], o_sb[:, j * P : (j + 1) * P], ident_f32[:])
+        def tanh_of_c(half, fb, c_out, o_sb):
             tanh_c = work.tile([P, HALF_BLOCKS, P], F32)
             nc.scalar.activation(out=tanh_c[:], in_=c_out[:], func=FUNC.Tanh)
+            return half, fb, tanh_c, o_sb
+
+        def finish(half, fb, tanh_c, o_sb):
+            o_t = flip_back(o_sb)
             h_out = stores.tile([P, HALF_BLOCKS, P], F32)
             nc.vector.tensor_tensor(out=h_out[:], in0=o_t[:], in1=tanh_c[:], op=ALU.mult)
-            rows = slice(HALF_BLOCKS * half, HALF_BLOCKS * (half + 1))
-            nc.sync.dma_start(out=out_rows[1, :, rows, fb * P : (fb + 1) * P], in_=h_out[:])
+            store(1, half, fb, h_out)
 
         def start_last(half, fb, c_sb, o_sb):
             c_parts = []
@@ -260,9 +266,7 @@ def tile_lstmcell_pa_kernel(
                         c_t[:, j, :], c_sb[:, block * P : (block + 1) * P], ident_f32[:]
                     )
                 c_parts.append(c_t)
-            o_t = psum.tile([P, HALF_BLOCKS, P], F32, tag="bank")
-            for j in range(HALF_BLOCKS):
-                nc.tensor.transpose(o_t[:, j, :], o_sb[:, j * P : (j + 1) * P], ident_f32[:])
+            o_t = flip_back(o_sb)
             tanh_parts = []
             for part in range(TAIL_PARTS):
                 tanh_c = work.tile([P, TAIL_BLOCKS, P], F32, name="tanh_last")
@@ -304,36 +308,55 @@ def tile_lstmcell_pa_kernel(
             flip_weight(EVEN_SHARES[gate], w_grouped, 0, gate)
             quantise_weight(0, w_grouped, gate - 1, 1)
         quantise_weight(0, w_grouped, GATES - 1, 1)
-        waiting = flip_weight_block(1, EVEN_SHARES)
+        waiting = grouped.tile([P, GATES, PASSES, P * PACK], BF16, name="w_grouped", align_bytes=64)
+        for gate in range(GATES):
+            flip_weight(EVEN_SHARES[gate], waiting, 1, gate)
 
         acted = None
         turned = None
         for half in range(HALVES):
             for fb in range(FEAT_BLOCKS):
                 last = half == HALVES - 1 and fb == FEAT_BLOCKS - 1
+                prepares = half == 0 and fb <= Z_STEP
                 z_block = fb - (Z_STEP - HALF_BLOCKS + 1) if half == 0 else -1
-                grouped_before, waiting = waiting, None
-                if grouped_before is not None:
-                    quantise_weight(fb + 1, grouped_before, 0, GATES // 2)
+                ready, waiting = waiting, None
+                if ready is not None:
+                    quantise_weight(fb + 1, ready, 0, GATES // 2)
                 if 0 <= z_block < HALF_BLOCKS:
                     add_z_block(1, z_block)
+                if ready is not None:
+                    quantise_weight(fb + 1, ready, GATES // 2, GATES // 2)
                 if half == 0 and fb == Z_STEP + 1:
                     quantise_z(1, 0, HALF_BLOCKS)
+                if half == 0 and fb < Z_STEP:
+                    waiting = grouped.tile(
+                        [P, GATES, PASSES, P * PACK], BF16, name="w_grouped", align_bytes=64
+                    )
 
-                def quantise_the_rest():
-                    if grouped_before is not None:
-                        quantise_weight(fb + 1, grouped_before, GATES // 2, GATES // 2)
+                def prepare(first, count):
+                    for piece in range(first, first + count):
+                        if fb < Z_STEP:
+                            flip_weight(PIPELINE_SHARES[piece], waiting, fb + 2, piece)
+                        else:
+                            flip_z_block(PIPELINE_SHARES[piece], 1, piece)
 
-                fresh = gates(half, fb, TAIL_PARTS if last else 1, quantise_the_rest)
-                newly_turned = turn_c(*acted) if acted is not None else None
+                newly_turned = None
+                ig_sb = first_gates(half, fb)
+                if prepares:
+                    if turned is not None:
+                        turned = tanh_of_c(*turned)
+                    if acted is not None:
+                        newly_turned = turn_c(*acted)
+                    prepare(0, GATES // 2)
+                fresh = last_gates(half, fb, ig_sb, TAIL_PARTS if last else 1)
+                if not prepares:
+                    newly_turned = turn_c(*acted)
+                    turned = tanh_of_c(*turned)
                 if turned is not None:
                     finish(*turned)
+                if prepares:
+                    prepare(GATES // 2, GATES // 2)
                 acted, turned = fresh, newly_turned
-                if half == 0 and fb + 2 < FEAT_BLOCKS:
-                    waiting = flip_weight_block(fb + 2, PIPELINE_SHARES)
-                if half == 0 and fb == Z_STEP:
-                    for j in range(HALF_BLOCKS):
-                        flip_z_block(PIPELINE_SHARES[j], 1, j)
         c_parts = start_last(*acted)
-        finish(*turned)
+        finish(*tanh_of_c(*turned))
         store_last_c(*c_parts)

@@ -29,6 +29,8 @@ Z_STEP = FEAT_BLOCKS - 2
 EVEN_SHARES = ("scalar", "vector", "scalar", "vector")
 PIPELINE_SHARES = ("vector", "scalar", "scalar", "scalar")
 
+RAW_BLOCKS = 6
+SORTED_GATES = (1, 3)
 TAIL_PARTS = 2
 TAIL_BLOCKS = HALF_BLOCKS // TAIL_PARTS
 
@@ -52,6 +54,8 @@ def tile_lstmcell_pa_kernel(
         const = ctx.enter_context(tc.tile_pool(name="const", bufs=1))
         resident = ctx.enter_context(tc.tile_pool(name="resident", bufs=1))
         grouped = ctx.enter_context(tc.tile_pool(name="grouped", bufs=2))
+        raw = ctx.enter_context(tc.tile_pool(name="raw", bufs=RAW_BLOCKS))
+        sorted_words = ctx.enter_context(tc.tile_pool(name="sorted_words", bufs=2 * len(SORTED_GATES)))
         work = ctx.enter_context(tc.tile_pool(name="work", bufs=2))
         stores = ctx.enter_context(tc.tile_pool(name="stores", bufs=4))
         psum = ctx.enter_context(tc.psum_pool(name="psum", bufs=PSUM_BANKS))
@@ -64,10 +68,7 @@ def tile_lstmcell_pa_kernel(
             resident.tile([P, HALF_BLOCKS, FEAT], BF16, name="s_sb%d" % half)
             for half in range(HALVES)
         ]
-        w_sb = [
-            resident.tile([P, GATES, FEAT], BF16, name="w_sb%d" % fb)
-            for fb in range(FEAT_BLOCKS)
-        ]
+        w_sb = [None] * FEAT_BLOCKS
         z_grouped = [
             resident.tile([P, PASSES, N_TILE, PACK], BF16, name="z_grouped%d" % half, align_bytes=64)
             for half in range(HALVES)
@@ -95,6 +96,7 @@ def tile_lstmcell_pa_kernel(
                 nc.sync.dma_start(out=s_sb[half][:, j, :], in_=s_rows[:, HALF_BLOCKS * half + j, :])
 
         def load_weight_block(fb):
+            w_sb[fb] = raw.tile([P, GATES, FEAT], BF16, name="w_raw")
             for gate in range(GATES):
                 nc.sync.dma_start(
                     out=w_sb[fb][:, gate, :], in_=weights[gate][fb * P : (fb + 1) * P, :]
@@ -104,7 +106,7 @@ def tile_lstmcell_pa_kernel(
         for fb in range(Z_STEP - 1):
             load_weight_block(fb)
         load_batch_half(1)
-        for fb in range(Z_STEP - 1, FEAT_BLOCKS):
+        for fb in range(Z_STEP - 1, RAW_BLOCKS):
             load_weight_block(fb)
 
         bias_rows = const.tile([P, P], BF16)
@@ -136,8 +138,15 @@ def tile_lstmcell_pa_kernel(
             nc.vector.tensor_copy(out=bias_sb[:], in_=bias_t[:, 0 : GATES * FEAT_BLOCKS])
             return bias_sb
 
-        def flip_words(src):
-            words = src.bitcast(F32).rearrange("p (g w u) -> p g u w", g=PASSES, u=2)
+        def words_of(src):
+            return src.bitcast(F32).rearrange("p (g w u) -> p g u w", g=PASSES, u=2)
+
+        def sort_weight(fb, gate):
+            planes = sorted_words.tile([P, PASSES, 2, P], F32, name="planes")
+            nc.vector.tensor_copy(out=planes[:], in_=words_of(w_sb[fb][:, gate, :]))
+            return planes[:]
+
+        def flip_words(words):
             flipped = psum.tile([P, PASSES * 2, P], F32, tag="bank")
             for plane in range(PASSES * 2):
                 nc.tensor.transpose(
@@ -154,7 +163,7 @@ def tile_lstmcell_pa_kernel(
             )
 
         def flip_z_block(engine, half, j):
-            z_t = flip_words(x_sb[half][:, j, :])
+            z_t = flip_words(words_of(x_sb[half][:, j, :]))
             interleave(
                 engine,
                 z_grouped[half][:, :, j * P : (j + 1) * P, :]
@@ -172,8 +181,8 @@ def tile_lstmcell_pa_kernel(
                     in_=z_grouped[half][:, g, cols, :].rearrange("p b t -> p (b t)"),
                 )
 
-        def flip_weight(engine, w_grouped, fb, gate):
-            w_t = flip_words(w_sb[fb][:, gate, :])
+        def flip_weight(engine, w_grouped, fb, gate, words):
+            w_t = flip_words(words)
             interleave(
                 engine,
                 w_grouped[:, gate, :, :].bitcast(F32).rearrange("p g (n u) -> p g n u", u=2),
@@ -301,16 +310,18 @@ def tile_lstmcell_pa_kernel(
             flip_z_block("scalar", 0, j)
         quantise_z(0, HALF_BLOCKS - 2, 1)
         w_grouped = grouped.tile([P, GATES, PASSES, P * PACK], BF16, align_bytes=64)
-        flip_weight("scalar", w_grouped, 0, 0)
+        flip_weight("scalar", w_grouped, 0, 0, words_of(w_sb[0][:, 0, :]))
         quantise_z(0, HALF_BLOCKS - 1, 1)
         bias_sb = flip_bias()
         for gate in range(1, GATES):
-            flip_weight(EVEN_SHARES[gate], w_grouped, 0, gate)
+            flip_weight(EVEN_SHARES[gate], w_grouped, 0, gate, words_of(w_sb[0][:, gate, :]))
             quantise_weight(0, w_grouped, gate - 1, 1)
         quantise_weight(0, w_grouped, GATES - 1, 1)
         waiting = grouped.tile([P, GATES, PASSES, P * PACK], BF16, name="w_grouped", align_bytes=64)
         for gate in range(GATES):
-            flip_weight(EVEN_SHARES[gate], waiting, 1, gate)
+            flip_weight(EVEN_SHARES[gate], waiting, 1, gate, words_of(w_sb[1][:, gate, :]))
+        for fb in range(RAW_BLOCKS, FEAT_BLOCKS):
+            load_weight_block(fb)
 
         acted = None
         turned = None
@@ -320,6 +331,13 @@ def tile_lstmcell_pa_kernel(
                 prepares = half == 0 and fb <= Z_STEP
                 z_block = fb - (Z_STEP - HALF_BLOCKS + 1) if half == 0 else -1
                 ready, waiting = waiting, None
+                words = []
+                if half == 0 and fb < Z_STEP:
+                    for gate in range(GATES):
+                        if gate in SORTED_GATES:
+                            words.append(sort_weight(fb + 2, gate))
+                        else:
+                            words.append(words_of(w_sb[fb + 2][:, gate, :]))
                 if ready is not None:
                     quantise_weight(fb + 1, ready, 0, GATES // 2)
                 if 0 <= z_block < HALF_BLOCKS:
@@ -336,7 +354,7 @@ def tile_lstmcell_pa_kernel(
                 def prepare(first, count):
                     for piece in range(first, first + count):
                         if fb < Z_STEP:
-                            flip_weight(PIPELINE_SHARES[piece], waiting, fb + 2, piece)
+                            flip_weight(PIPELINE_SHARES[piece], waiting, fb + 2, piece, words[piece])
                         else:
                             flip_z_block(PIPELINE_SHARES[piece], 1, piece)
 

from contextlib import ExitStack

import concourse.mybir as mybir
from concourse.masks import make_identity

F32 = mybir.dt.float32
BF16 = mybir.dt.bfloat16
U32 = mybir.dt.uint32
U8 = mybir.dt.uint8
FP8X4 = mybir.dt.float8_e4m3fn_x4
FUNC = mybir.ActivationFunctionType
ALU = mybir.AluOpType

P = 128
BATCH = 1024
FEAT = 1024
GATES = 4
PACK = 4
K_PASS = P * PACK
PASSES = FEAT // K_PASS
N_TILE = 512
HALVES = BATCH // N_TILE
HALF_BLOCKS = N_TILE // P
ROWS = BATCH // P
FEAT_BLOCKS = FEAT // P
PSUM_BANKS = 8
Z_STEP = FEAT_BLOCKS - 2

EVEN_SHARES = ("scalar", "vector", "scalar", "vector")
PIPELINE_SHARES = ("vector", "scalar", "scalar", "scalar")

RAW_BLOCKS = 6
SORTED_GATES = (1, 3)
TAIL_PARTS = 2
TAIL_BLOCKS = HALF_BLOCKS // TAIL_PARTS

FLOPS = 2 * BATCH * FEAT * GATES * FEAT


def tile_lstmcell_pa_kernel(
    tc, inputs, short_term_memory, Wf, b_f, Wi, b_i, Wg, b_g, Wo, b_o, out
):
    nc = tc.nc
    weights = (Wi, Wg, Wf, Wo)
    biases = (b_i, b_g, b_f, b_o)
    gate_funcs = (FUNC.Sigmoid, FUNC.Tanh, FUNC.Sigmoid, FUNC.Sigmoid)

    x_rows = inputs.rearrange("(p r) k -> p r k", r=ROWS)
    s_rows = short_term_memory.rearrange("(p r) k -> p r k", r=ROWS)
    out_rows = out.rearrange("s (p r) h -> s p r h", r=ROWS)

    with ExitStack() as ctx:
        ctx.enter_context(tc.manual_schedule())
        const = ctx.enter_context(tc.tile_pool(name="const", bufs=1))
        resident = ctx.enter_context(tc.tile_pool(name="resident", bufs=1))
        grouped = ctx.enter_context(tc.tile_pool(name="grouped", bufs=2))
        raw = ctx.enter_context(tc.tile_pool(name="raw", bufs=RAW_BLOCKS))
        sorted_words = ctx.enter_context(tc.tile_pool(name="sorted_words", bufs=2 * len(SORTED_GATES)))
        work = ctx.enter_context(tc.tile_pool(name="work", bufs=2))
        stores = ctx.enter_context(tc.tile_pool(name="stores", bufs=4))
        psum = ctx.enter_context(tc.psum_pool(name="psum", bufs=PSUM_BANKS))

        x_sb = [
            resident.tile([P, HALF_BLOCKS, FEAT], BF16, name="x_sb%d" % half)
            for half in range(HALVES)
        ]
        s_sb = [
            resident.tile([P, HALF_BLOCKS, FEAT], BF16, name="s_sb%d" % half)
            for half in range(HALVES)
        ]
        w_sb = [None] * FEAT_BLOCKS
        z_grouped = [
            resident.tile([P, PASSES, N_TILE, PACK], BF16, name="z_grouped%d" % half, align_bytes=64)
            for half in range(HALVES)
        ]
        z_codes = [
            resident.tile([P, PASSES, N_TILE], U32, name="z_codes%d" % half, align_bytes=64)
            for half in range(HALVES)
        ]
        z_scales = [
            resident.tile([P, PASSES, N_TILE], U8, name="z_scales%d" % half, align_bytes=64)
            for half in range(HALVES)
        ]
        w_codes = [
            resident.tile([P, GATES, PASSES, P], U32, name="w_codes%d" % fb, align_bytes=64)
            for fb in range(FEAT_BLOCKS)
        ]
        w_scales = [
            resident.tile([P, GATES, PASSES, P], U8, name="w_scales%d" % fb, align_bytes=64)
            for fb in range(FEAT_BLOCKS)
        ]

        def load_batch_half(half):
            for j in range(HALF_BLOCKS):
                nc.sync.dma_start(out=x_sb[half][:, j, :], in_=x_rows[:, HALF_BLOCKS * half + j, :])
                nc.sync.dma_start(out=s_sb[half][:, j, :], in_=s_rows[:, HALF_BLOCKS * half + j, :])

        def load_weight_block(fb):
            w_sb[fb] = raw.tile([P, GATES, FEAT], BF16, name="w_raw")
            for gate in range(GATES):
                nc.sync.dma_start(
                    out=w_sb[fb][:, gate, :], in_=weights[gate][fb * P : (fb + 1) * P, :]
                )

        load_batch_half(0)
        for fb in range(Z_STEP - 1):
            load_weight_block(fb)
        load_batch_half(1)
        for fb in range(Z_STEP - 1, RAW_BLOCKS):
            load_weight_block(fb)

        bias_rows = const.tile([P, P], BF16)
        nc.vector.memset(bias_rows[:], 0.0)
        for gate in range(GATES):
            nc.scalar.dma_start(
                out=bias_rows[gate * FEAT_BLOCKS : (gate + 1) * FEAT_BLOCKS, :],
                in_=biases[gate].rearrange("(r c) -> r c", c=P),
            )
        warm = const.tile([P, 1], F32)
        nc.vector.memset(warm[:], 0.0)
        nc.scalar.activation(out=warm[:], in_=warm[:], func=FUNC.Sigmoid)

        ident_bf = const.tile([P, P], BF16)
        make_identity(nc, ident_bf[:])
        ident_f32 = const.tile([P, P], F32)
        make_identity(nc, ident_f32[:])

        def copy_out(engine, out_ap, in_ap):
            if engine == "scalar":
                nc.scalar.copy(out=out_ap, in_=in_ap)
            else:
                nc.vector.tensor_copy(out=out_ap, in_=in_ap)

        def flip_bias():
            bias_t = psum.tile([P, P], BF16, tag="bank")
            nc.tensor.transpose(bias_t[:], bias_rows[:], ident_bf[:])
            bias_sb = const.tile([P, GATES * FEAT_BLOCKS], F32)
            nc.vector.tensor_copy(out=bias_sb[:], in_=bias_t[:, 0 : GATES * FEAT_BLOCKS])
            return bias_sb

        def words_of(src):
            return src.bitcast(F32).rearrange("p (g w u) -> p g u w", g=PASSES, u=2)

        def sort_weight(fb, gate):
            planes = sorted_words.tile([P, PASSES, 2, P], F32, name="planes")
            nc.vector.tensor_copy(out=planes[:], in_=words_of(w_sb[fb][:, gate, :]))
            return planes[:]

        def flip_words(words):
            flipped = psum.tile([P, PASSES * 2, P], F32, tag="bank")
            for plane in range(PASSES * 2):
                nc.tensor.transpose(
                    flipped[:, plane, :], words[:, plane // 2, plane % 2, :], ident_f32[:]
                )
            return flipped

        def interleave(engine, grouped_words, flipped):
            copy_out(engine, grouped_words, flipped[:].rearrange("p (g u) n -> p g n u", u=2))

        def add_z_block(half, j):
            nc.vector.tensor_tensor(
                out=x_sb[half][:, j, :], in0=x_sb[half][:, j, :], in1=s_sb[half][:, j, :], op=ALU.add
            )

        def flip_z_block(engine, half, j):
            z_t = flip_words(words_of(x_sb[half][:, j, :]))
            interleave(
                engine,
                z_grouped[half][:, :, j * P : (j + 1) * P, :]
                .rearrange("p g b t -> p g (b t)").bitcast(F32)
                .rearrange("p g (n u) -> p g n u", u=2),
                z_t,
            )

        def quantise_z(half, j, blocks):
            cols = slice(j * P, (j + blocks) * P)
            for g in range(PASSES):
                nc.vector.quantize_mx(
                    out=z_codes[half][:, g, cols].bitcast(FP8X4),
                    scales=z_scales[half][:, g, cols],
                    in_=z_grouped[half][:, g, cols, :].rearrange("p b t -> p (b t)"),
                )

        def flip_weight(engine, w_grouped, fb, gate, words):
            w_t = flip_words(words)
            interleave(
                engine,
                w_grouped[:, gate, :, :].bitcast(F32).rearrange("p g (n u) -> p g n u", u=2),
                w_t,
            )

        def quantise_weight(fb, w_grouped, gate, count):
            some = slice(gate, gate + count)
            nc.vector.quantize_mx(
                out=w_codes[fb][:, some, :, :].rearrange("p a g n -> p (a g n)").bitcast(FP8X4),
                scales=w_scales[fb][:, some, :, :].rearrange("p a g n -> p (a g n)"),
                in_=w_grouped[:, some, :, :].rearrange("p a g c -> p (a g c)"),
            )

        def gate_of(half, fb, gate):
            acc = psum.tile([P, N_TILE], F32, tag="bank")
            for g in range(PASSES):
                nc.tensor.matmul_mx(
                    out=acc[:],
                    lhsT=w_codes[fb][:, gate, g, :].bitcast(FP8X4),
                    lhsT_scale=w_scales[fb][:, gate, g, :],
                    rhs=z_codes[half][:, g, :].bitcast(FP8X4),
                    rhs_scale=z_scales[half][:, g, :],
                    start=(g == 0),
                    stop=(g == PASSES - 1),
                )
            gate_sb = work.tile(
                [P, N_TILE], F32, name="gate%d" % gate, bufs=(3 if gate == GATES - 1 else 2)
            )
            column = gate * FEAT_BLOCKS + fb
            nc.scalar.activation(
                out=gate_sb[:], in_=acc[:], func=gate_funcs[gate],
                bias=bias_sb[:, column : column + 1], scale=1.0,
            )
            return gate_sb

        def first_gates(half, fb):
            i_sb = gate_of(half, fb, 0)
            g_sb = gate_of(half, fb, 1)
            ig_sb = work.tile([P, N_TILE], F32)
            nc.vector.tensor_tensor(out=ig_sb[:], in0=i_sb[:], in1=g_sb[:], op=ALU.mult)
            return ig_sb

        def last_gates(half, fb, ig_sb, parts):
            f_sb = gate_of(half, fb, 2)
            o_sb = gate_of(half, fb, 3)
            c_sb = work.tile([P, N_TILE], F32)
            for part in range(parts):
                cols = slice(part * N_TILE // parts, (part + 1) * N_TILE // parts)
                nc.vector.tensor_tensor(
                    out=c_sb[:, cols], in0=f_sb[:, cols], in1=ig_sb[:, cols], op=ALU.add
                )
            return half, fb, c_sb, o_sb

        def flip_back(src):
            flipped = psum.tile([P, HALF_BLOCKS, P], F32, tag="bank")
            for j in range(HALF_BLOCKS):
                nc.tensor.transpose(flipped[:, j, :], src[:, j * P : (j + 1) * P], ident_f32[:])
            return flipped

        def store(which, half, fb, tile):
            rows = slice(HALF_BLOCKS * half, HALF_BLOCKS * (half + 1))
            nc.sync.dma_start(out=out_rows[which, :, rows, fb * P : (fb + 1) * P], in_=tile[:])

        def turn_c(half, fb, c_sb, o_sb):
            c_t = flip_back(c_sb)
            c_out = stores.tile([P, HALF_BLOCKS, P], F32)
            nc.vector.tensor_copy(out=c_out[:], in_=c_t[:])
            store(0, half, fb, c_out)
            return half, fb, c_out, o_sb

        def tanh_of_c(half, fb, c_out, o_sb):
            tanh_c = work.tile([P, HALF_BLOCKS, P], F32)
            nc.scalar.activation(out=tanh_c[:], in_=c_out[:], func=FUNC.Tanh)
            return half, fb, tanh_c, o_sb

        def finish(half, fb, tanh_c, o_sb):
            o_t = flip_back(o_sb)
            h_out = stores.tile([P, HALF_BLOCKS, P], F32)
            nc.vector.tensor_tensor(out=h_out[:], in0=o_t[:], in1=tanh_c[:], op=ALU.mult)
            store(1, half, fb, h_out)

        def start_last(half, fb, c_sb, o_sb):
            c_parts = []
            for part in range(TAIL_PARTS):
                c_t = psum.tile([P, TAIL_BLOCKS, P], F32, tag="bank")
                for j in range(TAIL_BLOCKS):
                    block = part * TAIL_BLOCKS + j
                    nc.tensor.transpose(
                        c_t[:, j, :], c_sb[:, block * P : (block + 1) * P], ident_f32[:]
                    )
                c_parts.append(c_t)
            o_t = flip_back(o_sb)
            tanh_parts = []
            for part in range(TAIL_PARTS):
                tanh_c = work.tile([P, TAIL_BLOCKS, P], F32, name="tanh_last")
                nc.scalar.activation(out=tanh_c[:], in_=c_parts[part][:], func=FUNC.Tanh)
                tanh_parts.append(tanh_c)
            for part in range(TAIL_PARTS):
                blocks = slice(part * TAIL_BLOCKS, (part + 1) * TAIL_BLOCKS)
                h_out = stores.tile([P, TAIL_BLOCKS, P], F32, name="h_last", bufs=2)
                nc.vector.tensor_tensor(
                    out=h_out[:], in0=o_t[:, blocks, :], in1=tanh_parts[part][:], op=ALU.mult
                )
                store_part(1, half, fb, part, h_out)
            return half, fb, c_parts

        def store_last_c(half, fb, c_parts):
            for part in range(TAIL_PARTS):
                c_out = stores.tile([P, TAIL_BLOCKS, P], F32, name="c_last", bufs=2)
                nc.scalar.copy(out=c_out[:], in_=c_parts[part][:])
                store_part(0, half, fb, part, c_out)

        def store_part(which, half, fb, part, tile):
            first = HALF_BLOCKS * half + TAIL_BLOCKS * part
            nc.sync.dma_start(
                out=out_rows[which, :, first : first + TAIL_BLOCKS, fb * P : (fb + 1) * P],
                in_=tile[:],
            )

        for j in range(HALF_BLOCKS):
            add_z_block(0, j)
            if j > 1:
                quantise_z(0, j - 2, 1)
            flip_z_block("scalar", 0, j)
        quantise_z(0, HALF_BLOCKS - 2, 1)
        w_grouped = grouped.tile([P, GATES, PASSES, P * PACK], BF16, align_bytes=64)
        flip_weight("scalar", w_grouped, 0, 0, words_of(w_sb[0][:, 0, :]))
        quantise_z(0, HALF_BLOCKS - 1, 1)
        bias_sb = flip_bias()
        for gate in range(1, GATES):
            flip_weight(EVEN_SHARES[gate], w_grouped, 0, gate, words_of(w_sb[0][:, gate, :]))
            quantise_weight(0, w_grouped, gate - 1, 1)
        quantise_weight(0, w_grouped, GATES - 1, 1)
        waiting = grouped.tile([P, GATES, PASSES, P * PACK], BF16, name="w_grouped", align_bytes=64)
        for gate in range(GATES):
            flip_weight(EVEN_SHARES[gate], waiting, 1, gate, words_of(w_sb[1][:, gate, :]))
        for fb in range(RAW_BLOCKS, FEAT_BLOCKS):
            load_weight_block(fb)

        acted = None
        turned = None
        for half in range(HALVES):
            for fb in range(FEAT_BLOCKS):
                last = half == HALVES - 1 and fb == FEAT_BLOCKS - 1
                prepares = half == 0 and fb <= Z_STEP
                z_block = fb - (Z_STEP - HALF_BLOCKS + 1) if half == 0 else -1
                ready, waiting = waiting, None
                words = []
                if half == 0 and fb < Z_STEP:
                    for gate in range(GATES):
                        if gate in SORTED_GATES:
                            words.append(sort_weight(fb + 2, gate))
                        else:
                            words.append(words_of(w_sb[fb + 2][:, gate, :]))
                if ready is not None:
                    quantise_weight(fb + 1, ready, 0, GATES // 2)
                if 0 <= z_block < HALF_BLOCKS:
                    add_z_block(1, z_block)
                if ready is not None:
                    quantise_weight(fb + 1, ready, GATES // 2, GATES // 2)
                if half == 0 and fb == Z_STEP + 1:
                    quantise_z(1, 0, HALF_BLOCKS)
                if half == 0 and fb < Z_STEP:
                    waiting = grouped.tile(
                        [P, GATES, PASSES, P * PACK], BF16, name="w_grouped", align_bytes=64
                    )

                def prepare(first, count):
                    for piece in range(first, first + count):
                        if fb < Z_STEP:
                            flip_weight(PIPELINE_SHARES[piece], waiting, fb + 2, piece, words[piece])
                        else:
                            flip_z_block(PIPELINE_SHARES[piece], 1, piece)

                newly_turned = None
                ig_sb = first_gates(half, fb)
                if prepares:
                    if turned is not None:
                        turned = tanh_of_c(*turned)
                    if acted is not None:
                        newly_turned = turn_c(*acted)
                    prepare(0, GATES // 2)
                fresh = last_gates(half, fb, ig_sb, TAIL_PARTS if last else 1)
                if not prepares:
                    newly_turned = turn_c(*acted)
                    turned = tanh_of_c(*turned)
                if turned is not None:
                    finish(*turned)
                if prepares:
                    prepare(GATES // 2, GATES // 2)
                acted, turned = fresh, newly_turned
        c_parts = start_last(*acted)
        finish(*tanh_of_c(*turned))
        store_last_c(*c_parts)
